import numpy as np
import ml_dtypes


def mxq(x, axis, fmt="e4m3"):
    dtype, down = {"e4m3": (ml_dtypes.float8_e4m3fn, 7), "e5m2": (ml_dtypes.float8_e5m2, 14)}[fmt]
    v = np.moveaxis(np.asarray(x, np.float32).astype(ml_dtypes.bfloat16).astype(np.float64), axis, -1)
    blocks = v.reshape(v.shape[:-1] + (-1, 32))
    amax = np.abs(blocks).max(-1, keepdims=True)
    byte = np.maximum(np.where(amax > 0, np.frexp(amax)[1] - 1 + 127, 0) - down, 1)
    scale = np.exp2(byte - 127.0)
    codes = (blocks / scale).astype(np.float32).astype(dtype).astype(np.float64)
    return np.moveaxis((codes * scale).reshape(v.shape), -1, axis)


WIDE = False


def mx_kscale(k):
    if not WIDE:
        return np.ones(k)
    levels = np.array([10, -10, 5, -5, 0])
    a = np.random.permutation(np.resize(levels, k // 512 * 4)).reshape(k // 512, 4)
    idx = np.arange(k)
    return np.exp2(a[idx // 512, idx % 128 // 32])


BF16 = ml_dtypes.bfloat16


def bf(x):
    return np.asarray(x, np.float32).astype(BF16)


def f64(x):
    return np.asarray(x).astype(np.float64)


T, M, HW, D, DK, H = 2, 512, 768, 1024, 1024, 8
EPS = 1e-6
EXTENT = 27.0


def rope_2d(x, pos):
    nt, n, c = x.shape
    half, quarter = c // 2, c // 4
    theta = 100.0 ** (-2.0 * np.arange(quarter) / half)

    def apply(part, p):
        fr = p[..., None] * theta
        cos, sin = np.cos(fr), np.sin(fr)
        pr = part.reshape(nt, n, quarter, 2)
        x1, x2 = pr[..., 0], pr[..., 1]
        return np.stack([x1 * cos - x2 * sin, x1 * sin + x2 * cos], axis=-1).reshape(nt, n, half)

    return np.concatenate([apply(x[:, :, :half], pos[..., 0]), apply(x[:, :, half:], pos[..., 1])], axis=-1)


def layernorm_nobias(x, gamma):
    mu = x.mean(-1, keepdims=True)
    var = ((x - mu) ** 2).mean(-1, keepdims=True)
    return (x - mu) / np.sqrt(var + EPS) * gamma


def setup_inputs():
    s = mx_kscale(D)
    return {"updated_track_tokens": bf(np.random.standard_normal((T, M, D)) * s),
            "tracks": bf(np.random.uniform(0.0, EXTENT, (T, M, 2))),
            "W_k": bf(np.random.standard_normal((DK, D)) / np.sqrt(D) / s),
            "k_gamma": bf(1.0 + 0.1 * np.random.standard_normal(DK))}


def reference(updated_track_tokens, tracks, W_k, k_gamma):
    k = mxq(f64(updated_track_tokens), 2, "e4m3") @ mxq(f64(W_k), 1, "e4m3").T
    k = rope_2d(k, f64(tracks))
    return layernorm_nobias(k, f64(k_gamma))

@@ -1,0 +1,208 @@
+import math
+from contextlib import ExitStack
+
+import concourse.mybir as mybir
+from concourse.masks import make_identity
+
+F32 = mybir.dt.float32
+BF16 = mybir.dt.bfloat16
+U32 = mybir.dt.uint32
+U8 = mybir.dt.uint8
+FP8X4 = mybir.dt.float8_e4m3fn_x4
+ALU = mybir.AluOpType
+ACT = mybir.ActivationFunctionType
+
+P = 128
+TOKENS = 1024
+D = 1024
+CHANNELS = 1024
+TILES = TOKENS // P
+K_PASS = 4 * P
+PASSES = D // K_PASS
+HALF = CHANNELS // 2
+PAIRS = HALF // 2
+DOUBLINGS = 8
+assert 2**DOUBLINGS == PAIRS
+W_BLOCKS = CHANNELS // (2 * P)
+WORDS = D // 2
+EPS = 1e-6
+THETA_BASE = 100.0
+TWO_PI = 2.0 * math.pi
+ROUND_MAGIC = 1.5 * 2.0**23
+
+FLOPS = 2 * TOKENS * D * CHANNELS
+
+
+def tile_attentionalsplatting_pa_kernel(tc, updated_track_tokens, tracks, W_k, k_gamma, out):
+    nc = tc.nc
+
+    x_dram = updated_track_tokens.flatten_outer_dims().rearrange("(p j) k -> p j k", j=TILES)
+    pos_dram = tracks.flatten_outer_dims().rearrange("(p j) c -> p (j c)", j=TILES)
+    w_dram = W_k.rearrange("(q p e) k -> q p (e k)", q=W_BLOCKS, p=P, e=2)
+    out_dram = out.flatten_outer_dims().rearrange("(p j) c -> p j c", j=TILES)
+
+    with ExitStack() as ctx:
+        keep = ctx.enter_context(tc.tile_pool(name="keep", bufs=1))
+        tables = ctx.enter_context(tc.tile_pool(name="tables", bufs=3))
+        work = ctx.enter_context(tc.tile_pool(name="work", bufs=2))
+        stats = ctx.enter_context(tc.tile_pool(name="stats", bufs=3))
+        flip_banks = ctx.enter_context(tc.psum_pool(name="flip_banks", bufs=4))
+        key_banks = ctx.enter_context(tc.psum_pool(name="key_banks", bufs=2))
+
+        pos_bf = keep.tile([P, 2 * TILES], BF16)
+        nc.sync.dma_start(out=pos_bf[:], in_=pos_dram)
+        w_raw = keep.tile([P, W_BLOCKS, 2, D], BF16)
+        for q in range(W_BLOCKS):
+            nc.sync.dma_start(out=w_raw[:, q].rearrange("p e k -> p (e k)"), in_=w_dram[q])
+        x_raw = keep.tile([P, TILES, D], BF16)
+        for j in range(0, TILES, 2):
+            nc.sync.dma_start(out=x_raw[:, j : j + 2, :], in_=x_dram[:, j : j + 2, :])
+        gamma = keep.tile([P, CHANNELS], BF16)
+        nc.sync.dma_start(out=gamma[:], in_=k_gamma.partition_broadcast(P))
+
+        ident = keep.tile([P, P], F32)
+        make_identity(nc, ident[:])
+        minus_half = keep.tile([P, 1], F32)
+        nc.vector.memset(minus_half[:], -0.5)
+        theta = keep.tile([P, PAIRS], F32)
+        nc.vector.memset(theta[:, 0:1], 1.0)
+        for w in [2**doubling for doubling in range(DOUBLINGS)]:
+            nc.vector.tensor_scalar_mul(
+                out=theta[:, w : 2 * w], in0=theta[:, 0:w], scalar1=THETA_BASE ** (-w / PAIRS)
+            )
+        pos = keep.tile([P, 2 * TILES], F32)
+        nc.vector.tensor_copy(out=pos[:], in_=pos_bf[:])
+
+        w_grouped = keep.tile([P, 2, PASSES * HALF * 4], BF16, align_bytes=64)
+        w_codes = keep.tile([P, 2, PASSES * HALF], U32, align_bytes=64)
+        w_scales = keep.tile([P, 2, PASSES * HALF], U8, align_bytes=64)
+        x_grouped = keep.tile([P, TILES, PASSES * P * 4], BF16, align_bytes=64)
+        x_codes = keep.tile([P, TILES, PASSES * P], U32, align_bytes=64)
+        x_scales = keep.tile([P, TILES, PASSES * P], U8, align_bytes=64)
+
+        def flip_rows(words, grouped_words, piece):
+            bank = flip_banks.tile([P, PASSES * 2 * P], F32, name="flip_bank")
+            for t in range(PASSES * 2):
+                nc.tensor.transpose(bank[:, t * P : (t + 1) * P], words[:, t * P : (t + 1) * P], ident[:])
+            planes = bank[:].rearrange("p (g u r) -> p g r u", g=PASSES, u=2)
+            if piece % 2 == 0:
+                nc.scalar.copy(out=grouped_words, in_=planes)
+            else:
+                nc.vector.tensor_copy(out=grouped_words, in_=planes)
+
+        def angle_tables(j):
+            turns = tables.tile([P, 2, PAIRS], F32, name="turns")
+            for h in range(2):
+                nc.vector.tensor_scalar(
+                    out=turns[:, h, :],
+                    in0=theta[:],
+                    scalar1=pos[:, 2 * j + h : 2 * j + h + 1],
+                    scalar2=1.0 / TWO_PI,
+                    op0=ALU.mult,
+                    op1=ALU.mult,
+                )
+            whole = tables.tile([P, 2, PAIRS], F32, name="whole")
+            nc.vector.tensor_scalar(
+                out=whole[:], in0=turns[:], scalar1=ROUND_MAGIC, scalar2=ROUND_MAGIC, op0=ALU.add, op1=ALU.subtract
+            )
+            frac = tables.tile([P, 2, PAIRS], F32, name="frac")
+            nc.vector.tensor_sub(out=frac[:], in0=turns[:], in1=whole[:])
+            sin = tables.tile([P, 2, PAIRS], F32, name="sin")
+            nc.scalar.activation(out=sin[:], in_=frac[:], func=ACT.Sin, scale=TWO_PI)
+            abs_frac = tables.tile([P, 2, PAIRS], F32, name="abs_frac")
+            nc.scalar.activation(out=abs_frac[:], in_=frac[:], func=ACT.Abs)
+            cos = tables.tile([P, 2, PAIRS], F32, name="cos")
+            nc.scalar.activation(out=cos[:], in_=abs_frac[:], func=ACT.Sin, scale=-TWO_PI, bias=math.pi / 2.0)
+            return cos, sin
+
+        def project(j):
+            halves = []
+            for h in range(2):
+                bank = key_banks.tile([P, HALF], F32, name="key_bank_%d" % h)
+                for g in range(PASSES):
+                    nc.tensor.matmul_mx(
+                        out=bank[:],
+                        lhsT=x_codes[:, j, g * P : (g + 1) * P].bitcast(FP8X4),
+                        lhsT_scale=x_scales[:, j, g * P : (g + 1) * P],
+                        rhs=w_codes[:, h, g * HALF : (g + 1) * HALF].bitcast(FP8X4),
+                        rhs_scale=w_scales[:, h, g * HALF : (g + 1) * HALF],
+                        start=(g == 0),
+                        stop=(g == PASSES - 1),
+                    )
+                halves.append(bank)
+            return halves
+
+        def rotate_and_normalise(j, halves, cos, sin):
+            k_cos = work.tile([P, 2, 2, PAIRS], F32, name="k_cos")
+            k_sin = work.tile([P, 2, 2, PAIRS], F32, name="k_sin")
+            for h in range(2):
+                planes = halves[h][:].rearrange("p (e i) -> p e i", e=2)
+                nc.vector.tensor_mul(
+                    out=k_cos[:, h], in0=planes, in1=cos[:, h, :].unsqueeze(1).to_broadcast([P, 2, PAIRS])
+                )
+                nc.vector.tensor_mul(
+                    out=k_sin[:, h], in0=planes, in1=sin[:, h, :].unsqueeze(1).to_broadcast([P, 2, PAIRS])
+                )
+            rotated = work.tile([P, 2, 2, PAIRS], F32, name="rotated")
+            sums = stats.tile([P, 2], F32, name="sums")
+            nc.vector.scalar_tensor_tensor(
+                out=rotated[:, :, 0, :], in0=k_cos[:, :, 0, :], scalar=1.0, in1=k_sin[:, :, 1, :],
+                op0=ALU.mult, op1=ALU.subtract, accum_out=sums[:, 0:1],
+            )
+            nc.vector.scalar_tensor_tensor(
+                out=rotated[:, :, 1, :], in0=k_cos[:, :, 1, :], scalar=1.0, in1=k_sin[:, :, 0, :],
+                op0=ALU.mult, op1=ALU.add, accum_out=sums[:, 1:2],
+            )
+            minus_mean = stats.tile([P, 1], F32, name="minus_mean")
+            nc.vector.tensor_scalar(
+                out=minus_mean[:], in0=sums[:, 0:1], scalar1=sums[:, 1:2], scalar2=-1.0 / CHANNELS,
+                op0=ALU.add, op1=ALU.mult,
+            )
+            squares = work.tile([P, CHANNELS], F32, name="squares")
+            sum_squares = stats.tile([P, 1], F32, name="sum_squares")
+            nc.scalar.activation(
+                out=squares[:], in_=rotated[:].rearrange("p h e i -> p (h e i)"), func=ACT.Square,
+                bias=minus_mean[:], scale=1.0, accum_out=sum_squares[:],
+            )
+            var_eps = stats.tile([P, 1], F32, name="var_eps")
+            nc.vector.tensor_scalar(
+                out=var_eps[:], in0=sum_squares[:], scalar1=1.0 / CHANNELS, scalar2=EPS, op0=ALU.mult, op1=ALU.add
+            )
+            rstd = stats.tile([P, 1], F32, name="rstd")
+            nc.gpsimd.tensor_tensor(out=rstd[:], in0=var_eps[:], in1=minus_half[:], op=ALU.pow)
+            shift = stats.tile([P, 1], F32, name="shift")
+            nc.vector.tensor_mul(out=shift[:], in0=minus_mean[:], in1=rstd[:])
+            normed = work.tile([P, CHANNELS], F32, name="normed")
+            nc.scalar.activation(
+                out=normed[:].rearrange("p (h i e) -> p h i e", h=2, e=2),
+                in_=rotated[:].rearrange("p h e i -> p h i e"),
+                func=ACT.Identity, bias=shift[:], scale=rstd[:],
+            )
+            result = work.tile([P, CHANNELS], F32, name="result")
+            nc.vector.tensor_mul(out=result[:], in0=normed[:], in1=gamma[:])
+            nc.sync.dma_start(out=out_dram[:, j, :], in_=result[:])
+
+        next_tables = angle_tables(0)
+
+        for q in range(W_BLOCKS):
+            h, b = divmod(q, W_BLOCKS // 2)
+            half_words = w_grouped[:, h, :].bitcast(F32).rearrange("p (g c u) -> p g c u", g=PASSES, u=2)
+            for e in range(2):
+                first = e * PAIRS + b * P
+                flip_rows(w_raw[:, q, e, :].bitcast(F32), half_words[:, :, first : first + P, :], piece=e)
+            if b == W_BLOCKS // 2 - 1:
+                nc.vector.quantize_mx(
+                    out=w_codes[:, h, :].bitcast(FP8X4), scales=w_scales[:, h, :], in_=w_grouped[:, h, :]
+                )
+
+        for j in range(TILES):
+            tile_words = x_grouped[:, j, :].bitcast(F32).rearrange("p (g r u) -> p g r u", g=PASSES, u=2)
+            flip_rows(x_raw[:, j, :].bitcast(F32), tile_words, piece=0)
+            nc.vector.quantize_mx(
+                out=x_codes[:, j, :].bitcast(FP8X4), scales=x_scales[:, j, :], in_=x_grouped[:, j, :]
+            )
+            halves = project(j)
+            cos, sin = next_tables
+            if j + 1 < TILES:
+                next_tables = angle_tables(j + 1)
+            rotate_and_normalise(j, halves, cos, sin)

@@ -43,11 +43,12 @@ def tile_attentionalsplatting_pa_kernel(tc, updated_track_tokens, tracks, W_k, k
 
     with ExitStack() as ctx:
         keep = ctx.enter_context(tc.tile_pool(name="keep", bufs=1))
-        tables = ctx.enter_context(tc.tile_pool(name="tables", bufs=3))
-        work = ctx.enter_context(tc.tile_pool(name="work", bufs=2))
-        stats = ctx.enter_context(tc.tile_pool(name="stats", bufs=3))
+        double = ctx.enter_context(tc.tile_pool(name="double", bufs=2))
+        triple = ctx.enter_context(tc.tile_pool(name="triple", bufs=3))
+        stats = ctx.enter_context(tc.tile_pool(name="stats", bufs=4))
         flip_banks = ctx.enter_context(tc.psum_pool(name="flip_banks", bufs=4))
         key_banks = ctx.enter_context(tc.psum_pool(name="key_banks", bufs=2))
+        ctx.enter_context(tc.manual_schedule())
 
         pos_bf = keep.tile([P, 2 * TILES], BF16)
         nc.sync.dma_start(out=pos_bf[:], in_=pos_dram)
@@ -57,8 +58,8 @@ def tile_attentionalsplatting_pa_kernel(tc, updated_track_tokens, tracks, W_k, k
         x_raw = keep.tile([P, TILES, D], BF16)
         for j in range(0, TILES, 2):
             nc.sync.dma_start(out=x_raw[:, j : j + 2, :], in_=x_dram[:, j : j + 2, :])
-        gamma = keep.tile([P, CHANNELS], BF16)
-        nc.sync.dma_start(out=gamma[:], in_=k_gamma.partition_broadcast(P))
+        gamma_bf = keep.tile([P, CHANNELS], BF16)
+        nc.sync.dma_start(out=gamma_bf[:], in_=k_gamma.partition_broadcast(P))
 
         ident = keep.tile([P, P], F32)
         make_identity(nc, ident[:])
@@ -72,6 +73,8 @@ def tile_attentionalsplatting_pa_kernel(tc, updated_track_tokens, tracks, W_k, k
             )
         pos = keep.tile([P, 2 * TILES], F32)
         nc.vector.tensor_copy(out=pos[:], in_=pos_bf[:])
+        gamma = keep.tile([P, CHANNELS], F32)
+        turns = keep.tile([P, 2 * TILES, PAIRS], F32)
 
         w_grouped = keep.tile([P, 2, PASSES * HALF * 4], BF16, align_bytes=64)
         w_codes = keep.tile([P, 2, PASSES * HALF], U32, align_bytes=64)
@@ -80,43 +83,74 @@ def tile_attentionalsplatting_pa_kernel(tc, updated_track_tokens, tracks, W_k, k
         x_codes = keep.tile([P, TILES, PASSES * P], U32, align_bytes=64)
         x_scales = keep.tile([P, TILES, PASSES * P], U8, align_bytes=64)
 
-        def flip_rows(words, grouped_words, piece):
+        frac_of, trig_of, keys_of, rotated_of, minus_mean_of = {}, {}, {}, {}, {}
+        sum_squares_of, rstd_of, shift_of, normed_of = {}, {}, {}, {}
+
+        def flip_rows(words, grouped_words, copy_engine):
             bank = flip_banks.tile([P, PASSES * 2 * P], F32, name="flip_bank")
             for t in range(PASSES * 2):
                 nc.tensor.transpose(bank[:, t * P : (t + 1) * P], words[:, t * P : (t + 1) * P], ident[:])
             planes = bank[:].rearrange("p (g u r) -> p g r u", g=PASSES, u=2)
-            if piece % 2 == 0:
+            if copy_engine == "scalar":
                 nc.scalar.copy(out=grouped_words, in_=planes)
             else:
                 nc.vector.tensor_copy(out=grouped_words, in_=planes)
 
-        def angle_tables(j):
-            turns = tables.tile([P, 2, PAIRS], F32, name="turns")
-            for h in range(2):
-                nc.vector.tensor_scalar(
-                    out=turns[:, h, :],
+        def flip_weights(q):
+            h, b = divmod(q, W_BLOCKS // 2)
+            half_words = w_grouped[:, h, :].bitcast(F32).rearrange("p (g c u) -> p g c u", g=PASSES, u=2)
+            for e, copy_engine in enumerate(["scalar", "vector"]):
+                first = e * PAIRS + b * P
+                flip_rows(w_raw[:, q, e, :].bitcast(F32), half_words[:, :, first : first + P, :], copy_engine)
+
+        def quantise_weights(h):
+            nc.vector.quantize_mx(
+                out=w_codes[:, h, :].bitcast(FP8X4), scales=w_scales[:, h, :], in_=w_grouped[:, h, :]
+            )
+
+        def flip_tokens(j):
+            tile_words = x_grouped[:, j, :].bitcast(F32).rearrange("p (g r u) -> p g r u", g=PASSES, u=2)
+            flip_rows(x_raw[:, j, :].bitcast(F32), tile_words, "scalar")
+
+        def quantise_tokens(j):
+            nc.vector.quantize_mx(
+                out=x_codes[:, j, :].bitcast(FP8X4), scales=x_scales[:, j, :], in_=x_grouped[:, j, :]
+            )
+
+        def angles_in_turns(engine, pair):
+            for column in range(4 * pair, 4 * pair + 4):
+                engine.tensor_scalar(
+                    out=turns[:, column, :],
                     in0=theta[:],
-                    scalar1=pos[:, 2 * j + h : 2 * j + h + 1],
+                    scalar1=pos[:, column : column + 1],
                     scalar2=1.0 / TWO_PI,
                     op0=ALU.mult,
                     op1=ALU.mult,
                 )
-            whole = tables.tile([P, 2, PAIRS], F32, name="whole")
+
+        def reduce_angles(pair):
+            pair_turns = turns[:, 4 * pair : 4 * pair + 4, :]
+            whole = keep.tile([P, 4, PAIRS], F32, name="whole")
             nc.vector.tensor_scalar(
-                out=whole[:], in0=turns[:], scalar1=ROUND_MAGIC, scalar2=ROUND_MAGIC, op0=ALU.add, op1=ALU.subtract
+                out=whole[:], in0=pair_turns, scalar1=ROUND_MAGIC, scalar2=ROUND_MAGIC, op0=ALU.add, op1=ALU.subtract
             )
-            frac = tables.tile([P, 2, PAIRS], F32, name="frac")
-            nc.vector.tensor_sub(out=frac[:], in0=turns[:], in1=whole[:])
-            sin = tables.tile([P, 2, PAIRS], F32, name="sin")
-            nc.scalar.activation(out=sin[:], in_=frac[:], func=ACT.Sin, scale=TWO_PI)
-            abs_frac = tables.tile([P, 2, PAIRS], F32, name="abs_frac")
-            nc.scalar.activation(out=abs_frac[:], in_=frac[:], func=ACT.Abs)
-            cos = tables.tile([P, 2, PAIRS], F32, name="cos")
-            nc.scalar.activation(out=cos[:], in_=abs_frac[:], func=ACT.Sin, scale=-TWO_PI, bias=math.pi / 2.0)
-            return cos, sin
+            frac = double.tile([P, 2, HALF], F32, name="frac")
+            nc.vector.tensor_sub(
+                out=frac[:].rearrange("p t (h i) -> p (t h) i", h=2), in0=pair_turns, in1=whole[:]
+            )
+            frac_of[pair] = frac
+            trig_of[pair] = double.tile([P, 2, 2, HALF], F32, name="trig")
+
+        def cos_and_sin(j):
+            frac = frac_of[j // 2][:, j % 2, :]
+            trig = trig_of[j // 2][:, j % 2]
+            nc.scalar.activation(out=trig[:, 1, :], in_=frac, func=ACT.Sin, scale=TWO_PI)
+            abs_frac = double.tile([P, HALF], F32, name="abs_frac")
+            nc.scalar.activation(out=abs_frac[:], in_=frac, func=ACT.Abs)
+            nc.scalar.activation(out=trig[:, 0, :], in_=abs_frac[:], func=ACT.Sin, scale=-TWO_PI, bias=math.pi / 2.0)
 
         def project(j):
-            halves = []
+            keys_of[j] = []
             for h in range(2):
                 bank = key_banks.tile([P, HALF], F32, name="key_bank_%d" % h)
                 for g in range(PASSES):
@@ -129,28 +163,26 @@ def tile_attentionalsplatting_pa_kernel(tc, updated_track_tokens, tracks, W_k, k
                         start=(g == 0),
                         stop=(g == PASSES - 1),
                     )
-                halves.append(bank)
-            return halves
+                keys_of[j].append(bank)
 
-        def rotate_and_normalise(j, halves, cos, sin):
-            k_cos = work.tile([P, 2, 2, PAIRS], F32, name="k_cos")
-            k_sin = work.tile([P, 2, 2, PAIRS], F32, name="k_sin")
+        def rotate(j):
+            trig = trig_of[j // 2][:, j % 2]
+            products = double.tile([P, 2, 2, 2, PAIRS], F32, name="products")
             for h in range(2):
-                planes = halves[h][:].rearrange("p (e i) -> p e i", e=2)
+                planes = keys_of[j][h][:].rearrange("p (e i) -> p e i", e=2)
                 nc.vector.tensor_mul(
-                    out=k_cos[:, h], in0=planes, in1=cos[:, h, :].unsqueeze(1).to_broadcast([P, 2, PAIRS])
+                    out=products[:, h],
+                    in0=planes.unsqueeze(1).to_broadcast([P, 2, 2, PAIRS]),
+                    in1=trig[:, :, h * PAIRS : (h + 1) * PAIRS].unsqueeze(2).to_broadcast([P, 2, 2, PAIRS]),
                 )
-                nc.vector.tensor_mul(
-                    out=k_sin[:, h], in0=planes, in1=sin[:, h, :].unsqueeze(1).to_broadcast([P, 2, PAIRS])
-                )
-            rotated = work.tile([P, 2, 2, PAIRS], F32, name="rotated")
+            rotated = triple.tile([P, 2, 2, PAIRS], F32, name="rotated")
             sums = stats.tile([P, 2], F32, name="sums")
             nc.vector.scalar_tensor_tensor(
-                out=rotated[:, :, 0, :], in0=k_cos[:, :, 0, :], scalar=1.0, in1=k_sin[:, :, 1, :],
+                out=rotated[:, :, 0, :], in0=products[:, :, 0, 0, :], scalar=1.0, in1=products[:, :, 1, 1, :],
                 op0=ALU.mult, op1=ALU.subtract, accum_out=sums[:, 0:1],
             )
             nc.vector.scalar_tensor_tensor(
-                out=rotated[:, :, 1, :], in0=k_cos[:, :, 1, :], scalar=1.0, in1=k_sin[:, :, 0, :],
+                out=rotated[:, :, 1, :], in0=products[:, :, 0, 1, :], scalar=1.0, in1=products[:, :, 1, 0, :],
                 op0=ALU.mult, op1=ALU.add, accum_out=sums[:, 1:2],
             )
             minus_mean = stats.tile([P, 1], F32, name="minus_mean")
@@ -158,51 +190,74 @@ def tile_attentionalsplatting_pa_kernel(tc, updated_track_tokens, tracks, W_k, k
                 out=minus_mean[:], in0=sums[:, 0:1], scalar1=sums[:, 1:2], scalar2=-1.0 / CHANNELS,
                 op0=ALU.add, op1=ALU.mult,
             )
-            squares = work.tile([P, CHANNELS], F32, name="squares")
-            sum_squares = stats.tile([P, 1], F32, name="sum_squares")
+            rotated_of[j], minus_mean_of[j] = rotated, minus_mean
+
+        def sum_of_squares(j):
+            squares = double.tile([P, CHANNELS], F32, name="squares")
+            sum_squares_of[j] = stats.tile([P, 1], F32, name="sum_squares")
             nc.scalar.activation(
-                out=squares[:], in_=rotated[:].rearrange("p h e i -> p (h e i)"), func=ACT.Square,
-                bias=minus_mean[:], scale=1.0, accum_out=sum_squares[:],
+                out=squares[:], in_=rotated_of[j][:].rearrange("p h e i -> p (h e i)"), func=ACT.Square,
+                bias=minus_mean_of[j][:], scale=1.0, accum_out=sum_squares_of[j][:],
             )
+
+        def scale_and_shift(j):
             var_eps = stats.tile([P, 1], F32, name="var_eps")
-            nc.vector.tensor_scalar(
-                out=var_eps[:], in0=sum_squares[:], scalar1=1.0 / CHANNELS, scalar2=EPS, op0=ALU.mult, op1=ALU.add
+            nc.gpsimd.tensor_scalar(
+                out=var_eps[:], in0=sum_squares_of[j][:], scalar1=1.0 / CHANNELS, scalar2=EPS,
+                op0=ALU.mult, op1=ALU.add,
             )
-            rstd = stats.tile([P, 1], F32, name="rstd")
-            nc.gpsimd.tensor_tensor(out=rstd[:], in0=var_eps[:], in1=minus_half[:], op=ALU.pow)
-            shift = stats.tile([P, 1], F32, name="shift")
-            nc.vector.tensor_mul(out=shift[:], in0=minus_mean[:], in1=rstd[:])
-            normed = work.tile([P, CHANNELS], F32, name="normed")
+            rstd_of[j] = stats.tile([P, 1], F32, name="rstd")
+            nc.gpsimd.tensor_tensor(out=rstd_of[j][:], in0=var_eps[:], in1=minus_half[:], op=ALU.pow)
+            shift_of[j] = stats.tile([P, 1], F32, name="shift")
+            nc.gpsimd.tensor_tensor(out=shift_of[j][:], in0=minus_mean_of[j][:], in1=rstd_of[j][:], op=ALU.mult)
+
+        def normalise(j):
+            normed_of[j] = double.tile([P, CHANNELS], F32, name="normed")
             nc.scalar.activation(
-                out=normed[:].rearrange("p (h i e) -> p h i e", h=2, e=2),
-                in_=rotated[:].rearrange("p h e i -> p h i e"),
-                func=ACT.Identity, bias=shift[:], scale=rstd[:],
+                out=normed_of[j][:].rearrange("p (h i e) -> p h i e", h=2, e=2),
+                in_=rotated_of[j][:].rearrange("p h e i -> p h i e"),
+                func=ACT.Identity, bias=shift_of[j][:], scale=rstd_of[j][:],
             )
-            result = work.tile([P, CHANNELS], F32, name="result")
-            nc.vector.tensor_mul(out=result[:], in0=normed[:], in1=gamma[:])
+
+        def apply_gamma_and_store(j):
+            engine = nc.vector if j == TILES - 1 else nc.gpsimd
+            result = triple.tile([P, CHANNELS], F32, name="result")
+            engine.tensor_tensor(out=result[:], in0=normed_of[j][:], in1=gamma[:], op=ALU.mult)
             nc.sync.dma_start(out=out_dram[:, j, :], in_=result[:])
 
-        next_tables = angle_tables(0)
-
+        angles_in_turns(nc.vector, 0)
+        for pair in range(1, TILES // 2):
+            angles_in_turns(nc.gpsimd, pair)
+        reduce_angles(0)
         for q in range(W_BLOCKS):
-            h, b = divmod(q, W_BLOCKS // 2)
-            half_words = w_grouped[:, h, :].bitcast(F32).rearrange("p (g c u) -> p g c u", g=PASSES, u=2)
-            for e in range(2):
-                first = e * PAIRS + b * P
-                flip_rows(w_raw[:, q, e, :].bitcast(F32), half_words[:, :, first : first + P, :], piece=e)
-            if b == W_BLOCKS // 2 - 1:
-                nc.vector.quantize_mx(
-                    out=w_codes[:, h, :].bitcast(FP8X4), scales=w_scales[:, h, :], in_=w_grouped[:, h, :]
-                )
+            flip_weights(q)
+            if q % 2 == 1:
+                quantise_weights(q // 2)
+        flip_tokens(0)
+        cos_and_sin(0)
+        flip_tokens(1)
+        quantise_tokens(0)
+        project(0)
+        reduce_angles(1)
+        cos_and_sin(1)
+        nc.gpsimd.tensor_scalar(out=gamma[:], in0=gamma_bf[:], scalar1=1.0, scalar2=0.0, op0=ALU.mult, op1=ALU.add)
 
-        for j in range(TILES):
-            tile_words = x_grouped[:, j, :].bitcast(F32).rearrange("p (g r u) -> p g r u", g=PASSES, u=2)
-            flip_rows(x_raw[:, j, :].bitcast(F32), tile_words, piece=0)
-            nc.vector.quantize_mx(
-                out=x_codes[:, j, :].bitcast(FP8X4), scales=x_scales[:, j, :], in_=x_grouped[:, j, :]
-            )
-            halves = project(j)
-            cos, sin = next_tables
-            if j + 1 < TILES:
-                next_tables = angle_tables(j + 1)
-            rotate_and_normalise(j, halves, cos, sin)
+        for s in range(TILES + 2):
+            if s + 2 < TILES:
+                flip_tokens(s + 2)
+            if s + 1 < TILES:
+                quantise_tokens(s + 1)
+                project(s + 1)
+            if 1 <= s <= TILES:
+                scale_and_shift(s - 1)
+            if s + 2 < TILES:
+                cos_and_sin(s + 2)
+            if 1 <= s <= TILES:
+                normalise(s - 1)
+            if s >= 2:
+                apply_gamma_and_store(s - 2)
+            if s < TILES:
+                rotate(s)
+                if s % 2 == 1 and s + 3 < TILES:
+                    reduce_angles((s + 3) // 2)
+                sum_of_squares(s)

@@ -30,6 +30,8 @@ THETA_BASE = 100.0
 TWO_PI = 2.0 * math.pi
 ROUND_MAGIC = 1.5 * 2.0**23
 
+LAST_TILES_ON_VECTOR = 2
+
 FLOPS = 2 * TOKENS * D * CHANNELS
 
 
@@ -220,7 +222,7 @@ def tile_attentionalsplatting_pa_kernel(tc, updated_track_tokens, tracks, W_k, k
             )
 
         def apply_gamma_and_store(j):
-            engine = nc.vector if j == TILES - 1 else nc.gpsimd
+            engine = nc.vector if j >= TILES - LAST_TILES_ON_VECTOR else nc.gpsimd
             result = triple.tile([P, CHANNELS], F32, name="result")
             engine.tensor_tensor(out=result[:], in0=normed_of[j][:], in1=gamma[:], op=ALU.mult)
             nc.sync.dma_start(out=out_dram[:, j, :], in_=result[:])
@@ -248,14 +250,14 @@ def tile_attentionalsplatting_pa_kernel(tc, updated_track_tokens, tracks, W_k, k
             if s + 1 < TILES:
                 quantise_tokens(s + 1)
                 project(s + 1)
+            if s >= 2:
+                apply_gamma_and_store(s - 2)
             if 1 <= s <= TILES:
                 scale_and_shift(s - 1)
             if s + 2 < TILES:
                 cos_and_sin(s + 2)
             if 1 <= s <= TILES:
                 normalise(s - 1)
-            if s >= 2:
-                apply_gamma_and_store(s - 2)
             if s < TILES:
                 rotate(s)
                 if s % 2 == 1 and s + 3 < TILES:

import math
from contextlib import ExitStack

import concourse.mybir as mybir
from concourse.masks import make_identity

F32 = mybir.dt.float32
BF16 = mybir.dt.bfloat16
U32 = mybir.dt.uint32
U8 = mybir.dt.uint8
FP8X4 = mybir.dt.float8_e4m3fn_x4
ALU = mybir.AluOpType
ACT = mybir.ActivationFunctionType

P = 128
TOKENS = 1024
D = 1024
CHANNELS = 1024
TILES = TOKENS // P
K_PASS = 4 * P
PASSES = D // K_PASS
HALF = CHANNELS // 2
PAIRS = HALF // 2
DOUBLINGS = 8
assert 2**DOUBLINGS == PAIRS
W_BLOCKS = CHANNELS // (2 * P)
WORDS = D // 2
EPS = 1e-6
THETA_BASE = 100.0
TWO_PI = 2.0 * math.pi
ROUND_MAGIC = 1.5 * 2.0**23

LAST_TILES_ON_VECTOR = 2

FLOPS = 2 * TOKENS * D * CHANNELS


def tile_attentionalsplatting_pa_kernel(tc, updated_track_tokens, tracks, W_k, k_gamma, out):
    nc = tc.nc

    x_dram = updated_track_tokens.flatten_outer_dims().rearrange("(p j) k -> p j k", j=TILES)
    pos_dram = tracks.flatten_outer_dims().rearrange("(p j) c -> p (j c)", j=TILES)
    w_dram = W_k.rearrange("(q p e) k -> q p (e k)", q=W_BLOCKS, p=P, e=2)
    out_dram = out.flatten_outer_dims().rearrange("(p j) c -> p j c", j=TILES)

    with ExitStack() as ctx:
        keep = ctx.enter_context(tc.tile_pool(name="keep", bufs=1))
        double = ctx.enter_context(tc.tile_pool(name="double", bufs=2))
        triple = ctx.enter_context(tc.tile_pool(name="triple", bufs=3))
        stats = ctx.enter_context(tc.tile_pool(name="stats", bufs=4))
        flip_banks = ctx.enter_context(tc.psum_pool(name="flip_banks", bufs=4))
        key_banks = ctx.enter_context(tc.psum_pool(name="key_banks", bufs=2))
        ctx.enter_context(tc.manual_schedule())

        pos_bf = keep.tile([P, 2 * TILES], BF16)
        nc.sync.dma_start(out=pos_bf[:], in_=pos_dram)
        w_raw = keep.tile([P, W_BLOCKS, 2, D], BF16)
        for q in range(W_BLOCKS):
            nc.sync.dma_start(out=w_raw[:, q].rearrange("p e k -> p (e k)"), in_=w_dram[q])
        x_raw = keep.tile([P, TILES, D], BF16)
        for j in range(0, TILES, 2):
            nc.sync.dma_start(out=x_raw[:, j : j + 2, :], in_=x_dram[:, j : j + 2, :])
        gamma_bf = keep.tile([P, CHANNELS], BF16)
        nc.sync.dma_start(out=gamma_bf[:], in_=k_gamma.partition_broadcast(P))

        ident = keep.tile([P, P], F32)
        make_identity(nc, ident[:])
        minus_half = keep.tile([P, 1], F32)
        nc.vector.memset(minus_half[:], -0.5)
        theta = keep.tile([P, PAIRS], F32)
        nc.vector.memset(theta[:, 0:1], 1.0)
        for w in [2**doubling for doubling in range(DOUBLINGS)]:
            nc.vector.tensor_scalar_mul(
                out=theta[:, w : 2 * w], in0=theta[:, 0:w], scalar1=THETA_BASE ** (-w / PAIRS)
            )
        pos = keep.tile([P, 2 * TILES], F32)
        nc.vector.tensor_copy(out=pos[:], in_=pos_bf[:])
        gamma = keep.tile([P, CHANNELS], F32)
        turns = keep.tile([P, 2 * TILES, PAIRS], F32)

        w_grouped = keep.tile([P, 2, PASSES * HALF * 4], BF16, align_bytes=64)
        w_codes = keep.tile([P, 2, PASSES * HALF], U32, align_bytes=64)
        w_scales = keep.tile([P, 2, PASSES * HALF], U8, align_bytes=64)
        x_grouped = keep.tile([P, TILES, PASSES * P * 4], BF16, align_bytes=64)
        x_codes = keep.tile([P, TILES, PASSES * P], U32, align_bytes=64)
        x_scales = keep.tile([P, TILES, PASSES * P], U8, align_bytes=64)

        frac_of, trig_of, keys_of, rotated_of, minus_mean_of = {}, {}, {}, {}, {}
        sum_squares_of, rstd_of, shift_of, normed_of = {}, {}, {}, {}

        def flip_rows(words, grouped_words, copy_engine):
            bank = flip_banks.tile([P, PASSES * 2 * P], F32, name="flip_bank")
            for t in range(PASSES * 2):
                nc.tensor.transpose(bank[:, t * P : (t + 1) * P], words[:, t * P : (t + 1) * P], ident[:])
            planes = bank[:].rearrange("p (g u r) -> p g r u", g=PASSES, u=2)
            if copy_engine == "scalar":
                nc.scalar.copy(out=grouped_words, in_=planes)
            else:
                nc.vector.tensor_copy(out=grouped_words, in_=planes)

        def flip_weights(q):
            h, b = divmod(q, W_BLOCKS // 2)
            half_words = w_grouped[:, h, :].bitcast(F32).rearrange("p (g c u) -> p g c u", g=PASSES, u=2)
            for e, copy_engine in enumerate(["scalar", "vector"]):
                first = e * PAIRS + b * P
                flip_rows(w_raw[:, q, e, :].bitcast(F32), half_words[:, :, first : first + P, :], copy_engine)

        def quantise_weights(h):
            nc.vector.quantize_mx(
                out=w_codes[:, h, :].bitcast(FP8X4), scales=w_scales[:, h, :], in_=w_grouped[:, h, :]
            )

        def flip_tokens(j):
            tile_words = x_grouped[:, j, :].bitcast(F32).rearrange("p (g r u) -> p g r u", g=PASSES, u=2)
            flip_rows(x_raw[:, j, :].bitcast(F32), tile_words, "scalar")

        def quantise_tokens(j):
            nc.vector.quantize_mx(
                out=x_codes[:, j, :].bitcast(FP8X4), scales=x_scales[:, j, :], in_=x_grouped[:, j, :]
            )

        def angles_in_turns(engine, pair):
            for column in range(4 * pair, 4 * pair + 4):
                engine.tensor_scalar(
                    out=turns[:, column, :],
                    in0=theta[:],
                    scalar1=pos[:, column : column + 1],
                    scalar2=1.0 / TWO_PI,
                    op0=ALU.mult,
                    op1=ALU.mult,
                )

        def reduce_angles(pair):
            pair_turns = turns[:, 4 * pair : 4 * pair + 4, :]
            whole = keep.tile([P, 4, PAIRS], F32, name="whole")
            nc.vector.tensor_scalar(
                out=whole[:], in0=pair_turns, scalar1=ROUND_MAGIC, scalar2=ROUND_MAGIC, op0=ALU.add, op1=ALU.subtract
            )
            frac = double.tile([P, 2, HALF], F32, name="frac")
            nc.vector.tensor_sub(
                out=frac[:].rearrange("p t (h i) -> p (t h) i", h=2), in0=pair_turns, in1=whole[:]
            )
            frac_of[pair] = frac
            trig_of[pair] = double.tile([P, 2, 2, HALF], F32, name="trig")

        def cos_and_sin(j):
            frac = frac_of[j // 2][:, j % 2, :]
            trig = trig_of[j // 2][:, j % 2]
            nc.scalar.activation(out=trig[:, 1, :], in_=frac, func=ACT.Sin, scale=TWO_PI)
            abs_frac = double.tile([P, HALF], F32, name="abs_frac")
            nc.scalar.activation(out=abs_frac[:], in_=frac, func=ACT.Abs)
            nc.scalar.activation(out=trig[:, 0, :], in_=abs_frac[:], func=ACT.Sin, scale=-TWO_PI, bias=math.pi / 2.0)

        def project(j):
            keys_of[j] = []
            for h in range(2):
                bank = key_banks.tile([P, HALF], F32, name="key_bank_%d" % h)
                for g in range(PASSES):
                    nc.tensor.matmul_mx(
                        out=bank[:],
                        lhsT=x_codes[:, j, g * P : (g + 1) * P].bitcast(FP8X4),
                        lhsT_scale=x_scales[:, j, g * P : (g + 1) * P],
                        rhs=w_codes[:, h, g * HALF : (g + 1) * HALF].bitcast(FP8X4),
                        rhs_scale=w_scales[:, h, g * HALF : (g + 1) * HALF],
                        start=(g == 0),
                        stop=(g == PASSES - 1),
                    )
                keys_of[j].append(bank)

        def rotate(j):
            trig = trig_of[j // 2][:, j % 2]
            products = double.tile([P, 2, 2, 2, PAIRS], F32, name="products")
            for h in range(2):
                planes = keys_of[j][h][:].rearrange("p (e i) -> p e i", e=2)
                nc.vector.tensor_mul(
                    out=products[:, h],
                    in0=planes.unsqueeze(1).to_broadcast([P, 2, 2, PAIRS]),
                    in1=trig[:, :, h * PAIRS : (h + 1) * PAIRS].unsqueeze(2).to_broadcast([P, 2, 2, PAIRS]),
                )
            rotated = triple.tile([P, 2, 2, PAIRS], F32, name="rotated")
            sums = stats.tile([P, 2], F32, name="sums")
            nc.vector.scalar_tensor_tensor(
                out=rotated[:, :, 0, :], in0=products[:, :, 0, 0, :], scalar=1.0, in1=products[:, :, 1, 1, :],
                op0=ALU.mult, op1=ALU.subtract, accum_out=sums[:, 0:1],
            )
            nc.vector.scalar_tensor_tensor(
                out=rotated[:, :, 1, :], in0=products[:, :, 0, 1, :], scalar=1.0, in1=products[:, :, 1, 0, :],
                op0=ALU.mult, op1=ALU.add, accum_out=sums[:, 1:2],
            )
            minus_mean = stats.tile([P, 1], F32, name="minus_mean")
            nc.vector.tensor_scalar(
                out=minus_mean[:], in0=sums[:, 0:1], scalar1=sums[:, 1:2], scalar2=-1.0 / CHANNELS,
                op0=ALU.add, op1=ALU.mult,
            )
            rotated_of[j], minus_mean_of[j] = rotated, minus_mean

        def sum_of_squares(j):
            squares = double.tile([P, CHANNELS], F32, name="squares")
            sum_squares_of[j] = stats.tile([P, 1], F32, name="sum_squares")
            nc.scalar.activation(
                out=squares[:], in_=rotated_of[j][:].rearrange("p h e i -> p (h e i)"), func=ACT.Square,
                bias=minus_mean_of[j][:], scale=1.0, accum_out=sum_squares_of[j][:],
            )

        def scale_and_shift(j):
            var_eps = stats.tile([P, 1], F32, name="var_eps")
            nc.gpsimd.tensor_scalar(
                out=var_eps[:], in0=sum_squares_of[j][:], scalar1=1.0 / CHANNELS, scalar2=EPS,
                op0=ALU.mult, op1=ALU.add,
            )
            rstd_of[j] = stats.tile([P, 1], F32, name="rstd")
            nc.gpsimd.tensor_tensor(out=rstd_of[j][:], in0=var_eps[:], in1=minus_half[:], op=ALU.pow)
            shift_of[j] = stats.tile([P, 1], F32, name="shift")
            nc.gpsimd.tensor_tensor(out=shift_of[j][:], in0=minus_mean_of[j][:], in1=rstd_of[j][:], op=ALU.mult)

        def normalise(j):
            normed_of[j] = double.tile([P, CHANNELS], F32, name="normed")
            nc.scalar.activation(
                out=normed_of[j][:].rearrange("p (h i e) -> p h i e", h=2, e=2),
                in_=rotated_of[j][:].rearrange("p h e i -> p h i e"),
                func=ACT.Identity, bias=shift_of[j][:], scale=rstd_of[j][:],
            )

        def apply_gamma_and_store(j):
            engine = nc.vector if j >= TILES - LAST_TILES_ON_VECTOR else nc.gpsimd
            result = triple.tile([P, CHANNELS], F32, name="result")
            engine.tensor_tensor(out=result[:], in0=normed_of[j][:], in1=gamma[:], op=ALU.mult)
            nc.sync.dma_start(out=out_dram[:, j, :], in_=result[:])

        angles_in_turns(nc.vector, 0)
        for pair in range(1, TILES // 2):
            angles_in_turns(nc.gpsimd, pair)
        reduce_angles(0)
        for q in range(W_BLOCKS):
            flip_weights(q)
            if q % 2 == 1:
                quantise_weights(q // 2)
        flip_tokens(0)
        cos_and_sin(0)
        flip_tokens(1)
        quantise_tokens(0)
        project(0)
        reduce_angles(1)
        cos_and_sin(1)
        nc.gpsimd.tensor_scalar(out=gamma[:], in0=gamma_bf[:], scalar1=1.0, scalar2=0.0, op0=ALU.mult, op1=ALU.add)

        for s in range(TILES + 2):
            if s + 2 < TILES:
                flip_tokens(s + 2)
            if s + 1 < TILES:
                quantise_tokens(s + 1)
                project(s + 1)
            if s >= 2:
                apply_gamma_and_store(s - 2)
            if 1 <= s <= TILES:
                scale_and_shift(s - 1)
            if s + 2 < TILES:
                cos_and_sin(s + 2)
            if 1 <= s <= TILES:
                normalise(s - 1)
            if s < TILES:
                rotate(s)
                if s % 2 == 1 and s + 3 < TILES:
                    reduce_angles((s + 3) // 2)
                sum_of_squares(s)
